import numpy as np
import ml_dtypes


def mxq(x, axis, fmt="e4m3"):
    dtype, down = {"e4m3": (ml_dtypes.float8_e4m3fn, 7), "e5m2": (ml_dtypes.float8_e5m2, 14)}[fmt]
    v = np.moveaxis(np.asarray(x, np.float32).astype(ml_dtypes.bfloat16).astype(np.float64), axis, -1)
    blocks = v.reshape(v.shape[:-1] + (-1, 32))
    amax = np.abs(blocks).max(-1, keepdims=True)
    byte = np.maximum(np.where(amax > 0, np.frexp(amax)[1] - 1 + 127, 0) - down, 1)
    scale = np.exp2(byte - 127.0)
    codes = (blocks / scale).astype(np.float32).astype(dtype).astype(np.float64)
    return np.moveaxis((codes * scale).reshape(v.shape), -1, axis)


WIDE = False


def mx_kscale(k):
    if not WIDE:
        return np.ones(k)
    levels = np.array([10, -10, 5, -5, 0])
    a = np.random.permutation(np.resize(levels, k // 512 * 4)).reshape(k // 512, 4)
    idx = np.arange(k)
    return np.exp2(a[idx // 512, idx % 128 // 32])


BF16 = ml_dtypes.bfloat16


def bf(x):
    return np.asarray(x, np.float32).astype(BF16)


def f64(x):
    return np.asarray(x).astype(np.float64)


E2M1 = np.array([0.0, 0.5, 1.0, 1.5, 2.0, 3.0, 4.0, 6.0, -0.0, -0.5, -1.0, -1.5, -2.0, -3.0, -4.0, -6.0])


def pack_weight(w, fmt):
    k, n = w.shape
    w = f64(bf(w)).reshape(k // 32, 32, n)
    amax = np.abs(w).max(1)
    if fmt == "e4m3":
        byte = np.frexp(amax)[1] - 1 + 127 - 7
    else:
        mant, ex = np.frexp(amax / 6.0)
        byte = np.where(mant > 0.5, ex, ex - 1) + 127
    byte = np.clip(np.where(amax > 0, byte, 1), 1, 254)
    scaled = (w * np.exp2(127.0 - byte)[:, None, :]).reshape(k, n).astype(np.float32)
    by_word = np.ascontiguousarray(scaled.reshape(k // 512, 128, 4, n).transpose(0, 1, 3, 2))
    if fmt == "e4m3":
        words = by_word.astype(ml_dtypes.float8_e4m3fn).view(np.uint8)
    else:
        c = by_word.astype(ml_dtypes.float4_e2m1fn).view(np.uint8) & 0xF
        words = c[..., 0::2] | (c[..., 1::2] << 4)
    return np.ascontiguousarray(words), np.ascontiguousarray(byte.astype(np.uint8).reshape(k // 512, 16, n))


def unpack_weight(words, scales, fmt):
    g, p, n, _ = words.shape
    if fmt == "e4m3":
        vals = np.ascontiguousarray(words).view(ml_dtypes.float8_e4m3fn).astype(np.float64)
    else:
        nib = np.empty((g, p, n, 4), np.uint8)
        nib[..., 0::2] = words & 0xF
        nib[..., 1::2] = words >> 4
        vals = E2M1[nib]
    vals = vals * np.repeat(np.exp2(scales.astype(np.float64) - 127.0), 8, axis=1)[..., None]
    return vals.transpose(0, 1, 3, 2).reshape(g * 512, n)

def pack4(w):
    words, scales = pack_weight(w, "e2m1")
    return words.reshape(words.shape[0], 128, -1), scales


def unpack4(words, scales):
    return unpack_weight(words.reshape(words.shape[0], 128, -1, 2), scales, "e2m1")


B, C, H, D, N, CO = 4, 128, 2048, 512, 4, 512
NC = N * C
EPS = 1e-5


def bn(v, gamma, beta, axes):
    mean = v.mean(axis=axes, keepdims=True)
    var = v.var(axis=axes, keepdims=True)
    return (v - mean) / np.sqrt(var + EPS) * gamma + beta


def setup_inputs():
    u = mx_kscale(NC)
    head = np.maximum(np.random.standard_normal((N, B, C, D)), 0.0) + 0.25 * np.random.standard_normal((N, B, C, D))
    w = np.random.standard_normal((CO, NC)) / np.sqrt(NC) / u[None, :]
    words, scales = pack4(np.ascontiguousarray(w.T))
    return {'head_res': bf(head * u.reshape(N, 1, C, 1)),
            'W_merge_words': words,
            'W_merge_scales': scales,
            'g_m': bf(1.0 + 0.1 * np.random.standard_normal(CO)),
            'b_m': bf(0.1 * np.random.standard_normal(CO))}


def reference(head_res, W_merge_words, W_merge_scales, g_m, b_m):
    cat = f64(head_res).transpose(1, 0, 2, 3).reshape(B, NC, D)
    m = unpack4(W_merge_words, W_merge_scales).T[None] @ mxq(cat, 1, 'e4m3')
    m = bn(m, f64(g_m)[None, :, None], f64(b_m)[None, :, None], (0, 2))
    return np.maximum(m, 0.0)

@@ -1,0 +1,131 @@
+from contextlib import ExitStack
+
+import concourse.mybir as mybir
+from concourse.masks import make_identity
+
+F32 = mybir.dt.float32
+BF16 = mybir.dt.bfloat16
+I32 = mybir.dt.int32
+U32 = mybir.dt.uint32
+U8 = mybir.dt.uint8
+FP8X4 = mybir.dt.float8_e4m3fn_x4
+FP4X4 = mybir.dt.float4_e2m1fn_x4
+ACT = mybir.ActivationFunctionType
+ALU = mybir.AluOpType
+
+HEADS, SAMPLES, CHANNELS, POSITIONS, OUT_CHANNELS = 4, 4, 128, 512, 512
+EPS = 1e-5
+P = 128
+PACK = 4
+HEAD_PARTS = CHANNELS // PACK
+OUT_TILES = OUT_CHANNELS // P
+RUN = 4
+RUNS = POSITIONS // RUN
+STATS = 6
+PSUM_BANKS = 8
+TILES_IN_PSUM = PSUM_BANKS // SAMPLES
+
+FLOPS = 2 * SAMPLES * OUT_CHANNELS * HEADS * CHANNELS * POSITIONS
+
+
+def tile_block_height_reducing_filtering_pb_kernel(
+    tc, head_res, W_merge_words, W_merge_scales, g_m, b_m, out
+):
+    nc = tc.nc
+    with ExitStack() as ctx:
+        keep = ctx.enter_context(tc.tile_pool(name="keep", bufs=1))
+        psum = ctx.enter_context(tc.psum_pool(name="psum", bufs=PSUM_BANKS))
+
+        w_words = keep.tile([P, 2 * OUT_CHANNELS], U8, align_bytes=64)
+        nc.sync.dma_start(out=w_words[:].bitcast(I32), in_=W_merge_words[0].bitcast(I32))
+        w_scales = keep.tile([P, OUT_CHANNELS], U8, align_bytes=64)
+        nc.vector.memset(w_scales[:].bitcast(I32), 0)
+        for quadrant in range(4):
+            nc.sync.dma_start(
+                out=w_scales[32 * quadrant : 32 * quadrant + 4, :].bitcast(I32),
+                in_=W_merge_scales[0, 4 * quadrant : 4 * quadrant + 4, :].bitcast(I32),
+            )
+
+        raw = [keep.tile([P, PACK * POSITIONS], BF16, name="raw%d" % b) for b in range(SAMPLES)]
+        for b in range(SAMPLES):
+            for head in (0, 2, 1, 3):
+                nc.sync.dma_start(
+                    out=raw[b][HEAD_PARTS * head : HEAD_PARTS * (head + 1), :],
+                    in_=head_res[head, b].rearrange("(q t) d -> q (t d)", t=PACK),
+                )
+
+        identity = keep.tile([P, P], BF16)
+        make_identity(nc, identity[:])
+        gb_rows = keep.tile([P, P], BF16)
+        nc.gpsimd.memset(gb_rows[:], 0.0)
+        nc.gpsimd.dma_start(out=gb_rows[0:OUT_TILES, :], in_=g_m.rearrange("(i c) -> i c", c=P))
+        nc.gpsimd.dma_start(
+            out=gb_rows[OUT_TILES : 2 * OUT_TILES, :], in_=b_m.rearrange("(i c) -> i c", c=P)
+        )
+        gb_bank = psum.tile([P, P], BF16, tag="bank")
+        nc.tensor.transpose(gb_bank[:], gb_rows[:], identity[:])
+        gamma_beta = keep.tile([P, 2 * OUT_TILES], F32)
+        nc.vector.tensor_copy(out=gamma_beta[:], in_=gb_bank[:, 0 : 2 * OUT_TILES])
+
+        eps = keep.tile([P, 1], F32)
+        nc.vector.memset(eps[:], EPS)
+        table_warmer = keep.tile([P, 1], F32)
+        nc.scalar.activation(out=table_warmer[:], in_=eps[:], func=ACT.Sqrt)
+
+        codes = [keep.tile([P, POSITIONS], U32, name="codes%d" % b, align_bytes=64) for b in range(SAMPLES)]
+        scales = [keep.tile([P, POSITIONS], U8, name="scales%d" % b, align_bytes=64) for b in range(SAMPLES)]
+        banks = {}
+
+        def multiply(i, b):
+            banks[i, b] = psum.tile([P, POSITIONS], F32, tag="bank", name="m%d_%d" % (i, b))
+            nc.tensor.matmul_mx(
+                out=banks[i, b][:],
+                lhsT=w_words[:, 2 * P * i : 2 * P * (i + 1)].bitcast(FP4X4),
+                lhsT_scale=w_scales[:, P * i : P * (i + 1)],
+                rhs=codes[b][:].bitcast(FP8X4),
+                rhs_scale=scales[b][:],
+                start=True,
+                stop=True,
+            )
+
+        for b in range(SAMPLES):
+            grouped = keep.tile([P, POSITIONS * PACK], BF16, name="grouped%d" % b, align_bytes=64)
+            by_run_in = raw[b][:].rearrange("p (t c i) -> p c t i", t=PACK, i=RUN)
+            by_run_out = grouped[:].rearrange("p (c i t) -> p c t i", i=RUN, t=PACK)
+            nc.vector.tensor_copy(out=by_run_out[:, 0 : RUNS // 2], in_=by_run_in[:, 0 : RUNS // 2])
+            nc.scalar.copy(out=by_run_out[:, RUNS // 2 : RUNS], in_=by_run_in[:, RUNS // 2 : RUNS])
+            nc.vector.quantize_mx(out=codes[b][:].bitcast(FP8X4), scales=scales[b][:], in_=grouped[:])
+            for i in range(TILES_IN_PSUM):
+                multiply(i, b)
+
+        for i in range(OUT_TILES):
+            stats = keep.tile([P, SAMPLES * STATS], F32, name="stats%d" % i)
+            for b in range(SAMPLES):
+                nc.vector.bn_stats(out=stats[:, STATS * b : STATS * (b + 1)], in_=banks[i, b][:])
+            mean_var = keep.tile([P, 2], F32, name="mean_var%d" % i)
+            nc.vector.bn_aggr(out=mean_var[:], in_=stats[:])
+            std = keep.tile([P, 1], F32, name="std%d" % i)
+            nc.scalar.activation(out=std[:], in_=mean_var[:, 1:2], func=ACT.Sqrt, bias=eps[:], scale=1.0)
+            minus_mean = keep.tile([P, 1], F32, name="minus_mean%d" % i)
+            nc.vector.tensor_scalar_mul(out=minus_mean[:], in0=mean_var[:, 0:1], scalar1=-1.0)
+            rstd = keep.tile([P, 1], F32, name="rstd%d" % i)
+            nc.vector.reciprocal(out=rstd[:], in_=std[:])
+            gain = keep.tile([P, 1], F32, name="gain%d" % i)
+            nc.vector.tensor_mul(out=gain[:], in0=rstd[:], in1=gamma_beta[:, i : i + 1])
+            shift = keep.tile([P, 1], F32, name="shift%d" % i)
+            nc.vector.tensor_scalar(
+                out=shift[:],
+                in0=minus_mean[:],
+                scalar1=gain[:],
+                scalar2=gamma_beta[:, OUT_TILES + i : OUT_TILES + i + 1],
+                op0=ALU.mult,
+                op1=ALU.add,
+            )
+            for b in range(SAMPLES):
+                result = keep.tile([P, POSITIONS], F32, name="result%d_%d" % (i, b))
+                nc.scalar.activation(
+                    out=result[:], in_=banks[i, b][:], func=ACT.Relu, bias=shift[:], scale=gain[:]
+                )
+                nc.sync.dma_start(out=out[b, P * i : P * (i + 1), :], in_=result[:])
+                if i + TILES_IN_PSUM < OUT_TILES:
+                    multiply(i + TILES_IN_PSUM, b)

@@ -35,11 +35,17 @@ def tile_block_height_reducing_filtering_pb_kernel(
     with ExitStack() as ctx:
         keep = ctx.enter_context(tc.tile_pool(name="keep", bufs=1))
         psum = ctx.enter_context(tc.psum_pool(name="psum", bufs=PSUM_BANKS))
+        ctx.enter_context(tc.manual_schedule())
+
+        gb_rows = keep.tile([P, P], BF16)
+        nc.vector.memset(gb_rows[:], 0.0)
+        w_scales = keep.tile([P, OUT_CHANNELS], U8, align_bytes=64)
+        nc.vector.memset(w_scales[:].bitcast(I32), 0)
+        eps = keep.tile([P, 1], F32)
+        nc.vector.memset(eps[:], EPS)
 
         w_words = keep.tile([P, 2 * OUT_CHANNELS], U8, align_bytes=64)
         nc.sync.dma_start(out=w_words[:].bitcast(I32), in_=W_merge_words[0].bitcast(I32))
-        w_scales = keep.tile([P, OUT_CHANNELS], U8, align_bytes=64)
-        nc.vector.memset(w_scales[:].bitcast(I32), 0)
         for quadrant in range(4):
             nc.sync.dma_start(
                 out=w_scales[32 * quadrant : 32 * quadrant + 4, :].bitcast(I32),
@@ -54,27 +60,36 @@ def tile_block_height_reducing_filtering_pb_kernel(
                     in_=head_res[head, b].rearrange("(q t) d -> q (t d)", t=PACK),
                 )
 
-        identity = keep.tile([P, P], BF16)
-        make_identity(nc, identity[:])
-        gb_rows = keep.tile([P, P], BF16)
-        nc.gpsimd.memset(gb_rows[:], 0.0)
         nc.gpsimd.dma_start(out=gb_rows[0:OUT_TILES, :], in_=g_m.rearrange("(i c) -> i c", c=P))
         nc.gpsimd.dma_start(
             out=gb_rows[OUT_TILES : 2 * OUT_TILES, :], in_=b_m.rearrange("(i c) -> i c", c=P)
         )
+        identity = keep.tile([P, P], BF16)
+        make_identity(nc, identity[:])
         gb_bank = psum.tile([P, P], BF16, tag="bank")
         nc.tensor.transpose(gb_bank[:], gb_rows[:], identity[:])
-        gamma_beta = keep.tile([P, 2 * OUT_TILES], F32)
-        nc.vector.tensor_copy(out=gamma_beta[:], in_=gb_bank[:, 0 : 2 * OUT_TILES])
-
-        eps = keep.tile([P, 1], F32)
-        nc.vector.memset(eps[:], EPS)
         table_warmer = keep.tile([P, 1], F32)
-        nc.scalar.activation(out=table_warmer[:], in_=eps[:], func=ACT.Sqrt)
+        nc.scalar.activation(out=table_warmer[:], in_=eps[:], func=ACT.Abs_reciprocal_sqrt)
+        gamma_beta = keep.tile([P, 2 * OUT_TILES], F32)
+        nc.scalar.copy(out=gamma_beta[:], in_=gb_bank[:, 0 : 2 * OUT_TILES])
 
         codes = [keep.tile([P, POSITIONS], U32, name="codes%d" % b, align_bytes=64) for b in range(SAMPLES)]
         scales = [keep.tile([P, POSITIONS], U8, name="scales%d" % b, align_bytes=64) for b in range(SAMPLES)]
         banks = {}
+        stats = [keep.tile([P, SAMPLES * STATS], F32, name="stats%d" % i) for i in range(OUT_TILES)]
+        mean_var = [keep.tile([P, 2], F32, name="mean_var%d" % i) for i in range(OUT_TILES)]
+        rstd = [keep.tile([P, 1], F32, name="rstd%d" % i) for i in range(OUT_TILES)]
+        minus_mean_gamma = [keep.tile([P, 1], F32, name="minus_mean_gamma%d" % i) for i in range(OUT_TILES)]
+        gain = [keep.tile([P, 1], F32, name="gain%d" % i) for i in range(OUT_TILES)]
+        shift = [keep.tile([P, 1], F32, name="shift%d" % i) for i in range(OUT_TILES)]
+
+        def quantise(b):
+            grouped = keep.tile([P, POSITIONS * PACK], BF16, name="grouped%d" % b, align_bytes=64)
+            by_run_in = raw[b][:].rearrange("p (t c i) -> p c t i", t=PACK, i=RUN)
+            by_run_out = grouped[:].rearrange("p (c i t) -> p c t i", i=RUN, t=PACK)
+            nc.vector.tensor_copy(out=by_run_out[:, 0 : RUNS // 2], in_=by_run_in[:, 0 : RUNS // 2])
+            nc.scalar.copy(out=by_run_out[:, RUNS // 2 : RUNS], in_=by_run_in[:, RUNS // 2 : RUNS])
+            nc.vector.quantize_mx(out=codes[b][:].bitcast(FP8X4), scales=scales[b][:], in_=grouped[:])
 
         def multiply(i, b):
             banks[i, b] = psum.tile([P, POSITIONS], F32, tag="bank", name="m%d_%d" % (i, b))
@@ -88,44 +103,60 @@ def tile_block_height_reducing_filtering_pb_kernel(
                 stop=True,
             )
 
-        for b in range(SAMPLES):
-            grouped = keep.tile([P, POSITIONS * PACK], BF16, name="grouped%d" % b, align_bytes=64)
-            by_run_in = raw[b][:].rearrange("p (t c i) -> p c t i", t=PACK, i=RUN)
-            by_run_out = grouped[:].rearrange("p (c i t) -> p c t i", i=RUN, t=PACK)
-            nc.vector.tensor_copy(out=by_run_out[:, 0 : RUNS // 2], in_=by_run_in[:, 0 : RUNS // 2])
-            nc.scalar.copy(out=by_run_out[:, RUNS // 2 : RUNS], in_=by_run_in[:, RUNS // 2 : RUNS])
-            nc.vector.quantize_mx(out=codes[b][:].bitcast(FP8X4), scales=scales[b][:], in_=grouped[:])
-            for i in range(TILES_IN_PSUM):
-                multiply(i, b)
+        def statistics(i, b):
+            nc.vector.bn_stats(out=stats[i][:, STATS * b : STATS * (b + 1)], in_=banks[i, b][:])
 
-        for i in range(OUT_TILES):
-            stats = keep.tile([P, SAMPLES * STATS], F32, name="stats%d" % i)
-            for b in range(SAMPLES):
-                nc.vector.bn_stats(out=stats[:, STATS * b : STATS * (b + 1)], in_=banks[i, b][:])
-            mean_var = keep.tile([P, 2], F32, name="mean_var%d" % i)
-            nc.vector.bn_aggr(out=mean_var[:], in_=stats[:])
-            std = keep.tile([P, 1], F32, name="std%d" % i)
-            nc.scalar.activation(out=std[:], in_=mean_var[:, 1:2], func=ACT.Sqrt, bias=eps[:], scale=1.0)
-            minus_mean = keep.tile([P, 1], F32, name="minus_mean%d" % i)
-            nc.vector.tensor_scalar_mul(out=minus_mean[:], in0=mean_var[:, 0:1], scalar1=-1.0)
-            rstd = keep.tile([P, 1], F32, name="rstd%d" % i)
-            nc.vector.reciprocal(out=rstd[:], in_=std[:])
-            gain = keep.tile([P, 1], F32, name="gain%d" % i)
-            nc.vector.tensor_mul(out=gain[:], in0=rstd[:], in1=gamma_beta[:, i : i + 1])
-            shift = keep.tile([P, 1], F32, name="shift%d" % i)
+        def moments(i):
+            nc.vector.bn_aggr(out=mean_var[i][:], in_=stats[i][:])
+            nc.scalar.activation(
+                out=rstd[i][:], in_=mean_var[i][:, 1:2], func=ACT.Abs_reciprocal_sqrt, bias=eps[:], scale=1.0
+            )
             nc.vector.tensor_scalar(
-                out=shift[:],
-                in0=minus_mean[:],
-                scalar1=gain[:],
+                out=minus_mean_gamma[i][:],
+                in0=mean_var[i][:, 0:1],
+                scalar1=gamma_beta[:, i : i + 1],
+                scalar2=-1.0,
+                op0=ALU.mult,
+                op1=ALU.mult,
+            )
+
+        def coefficients(i):
+            nc.vector.tensor_mul(out=gain[i][:], in0=rstd[i][:], in1=gamma_beta[:, i : i + 1])
+            nc.vector.tensor_scalar(
+                out=shift[i][:],
+                in0=rstd[i][:],
+                scalar1=minus_mean_gamma[i][:],
                 scalar2=gamma_beta[:, OUT_TILES + i : OUT_TILES + i + 1],
                 op0=ALU.mult,
                 op1=ALU.add,
             )
+
+        def normalise(i, b):
+            result = keep.tile([P, POSITIONS], F32, name="result%d_%d" % (i, b))
+            nc.scalar.activation(
+                out=result[:], in_=banks[i, b][:], func=ACT.Relu, bias=shift[i][:], scale=gain[i][:]
+            )
+            nc.sync.dma_start(out=out[b, P * i : P * (i + 1), :], in_=result[:])
+
+        for b in range(SAMPLES):
+            quantise(b)
+            for i in range(TILES_IN_PSUM):
+                multiply(i, b)
+            if b > 0:
+                statistics(0, b - 1)
+        statistics(0, SAMPLES - 1)
+        moments(0)
+
+        for i in range(OUT_TILES):
+            following = i + 1
+            if following < OUT_TILES:
+                statistics(following, 0)
+            coefficients(i)
             for b in range(SAMPLES):
-                result = keep.tile([P, POSITIONS], F32, name="result%d_%d" % (i, b))
-                nc.scalar.activation(
-                    out=result[:], in_=banks[i, b][:], func=ACT.Relu, bias=shift[:], scale=gain[:]
-                )
-                nc.sync.dma_start(out=out[b, P * i : P * (i + 1), :], in_=result[:])
+                normalise(i, b)
                 if i + TILES_IN_PSUM < OUT_TILES:
                     multiply(i + TILES_IN_PSUM, b)
+                if following < OUT_TILES and b + 1 < SAMPLES:
+                    statistics(following, b + 1)
+                if following < OUT_TILES and b + 2 == SAMPLES:
+                    moments(following)

@@ -21,6 +21,7 @@ HEAD_PARTS = CHANNELS // PACK
 OUT_TILES = OUT_CHANNELS // P
 RUN = 4
 RUNS = POSITIONS // RUN
+VECTOR_RUNS = 48
 STATS = 6
 PSUM_BANKS = 8
 TILES_IN_PSUM = PSUM_BANKS // SAMPLES
@@ -37,15 +38,8 @@ def tile_block_height_reducing_filtering_pb_kernel(
         psum = ctx.enter_context(tc.psum_pool(name="psum", bufs=PSUM_BANKS))
         ctx.enter_context(tc.manual_schedule())
 
-        gb_rows = keep.tile([P, P], BF16)
-        nc.vector.memset(gb_rows[:], 0.0)
         w_scales = keep.tile([P, OUT_CHANNELS], U8, align_bytes=64)
         nc.vector.memset(w_scales[:].bitcast(I32), 0)
-        eps = keep.tile([P, 1], F32)
-        nc.vector.memset(eps[:], EPS)
-
-        w_words = keep.tile([P, 2 * OUT_CHANNELS], U8, align_bytes=64)
-        nc.sync.dma_start(out=w_words[:].bitcast(I32), in_=W_merge_words[0].bitcast(I32))
         for quadrant in range(4):
             nc.sync.dma_start(
                 out=w_scales[32 * quadrant : 32 * quadrant + 4, :].bitcast(I32),
@@ -53,25 +47,37 @@ def tile_block_height_reducing_filtering_pb_kernel(
             )
 
         raw = [keep.tile([P, PACK * POSITIONS], BF16, name="raw%d" % b) for b in range(SAMPLES)]
-        for b in range(SAMPLES):
+
+        def load(b):
             for head in (0, 2, 1, 3):
                 nc.sync.dma_start(
                     out=raw[b][HEAD_PARTS * head : HEAD_PARTS * (head + 1), :],
                     in_=head_res[head, b].rearrange("(q t) d -> q (t d)", t=PACK),
                 )
 
+        load(0)
+        w_words = keep.tile([P, 2 * OUT_CHANNELS], U8, align_bytes=64)
+        nc.sync.dma_start(out=w_words[:].bitcast(I32), in_=W_merge_words[0].bitcast(I32))
+        for b in range(1, SAMPLES):
+            load(b)
+
+        gb_rows = keep.tile([P, P], BF16)
+        nc.vector.memset(gb_rows[:], 0.0)
         nc.gpsimd.dma_start(out=gb_rows[0:OUT_TILES, :], in_=g_m.rearrange("(i c) -> i c", c=P))
         nc.gpsimd.dma_start(
             out=gb_rows[OUT_TILES : 2 * OUT_TILES, :], in_=b_m.rearrange("(i c) -> i c", c=P)
         )
         identity = keep.tile([P, P], BF16)
-        make_identity(nc, identity[:])
+        nc.vector.memset(identity[:], 0.0)
+        make_identity(nc, identity[:], nomemset=True)
         gb_bank = psum.tile([P, P], BF16, tag="bank")
         nc.tensor.transpose(gb_bank[:], gb_rows[:], identity[:])
+        gamma_beta = keep.tile([P, 2 * OUT_TILES], F32)
+
+        eps = keep.tile([P, 1], F32)
+        nc.vector.memset(eps[:], EPS)
         table_warmer = keep.tile([P, 1], F32)
         nc.scalar.activation(out=table_warmer[:], in_=eps[:], func=ACT.Abs_reciprocal_sqrt)
-        gamma_beta = keep.tile([P, 2 * OUT_TILES], F32)
-        nc.scalar.copy(out=gamma_beta[:], in_=gb_bank[:, 0 : 2 * OUT_TILES])
 
         codes = [keep.tile([P, POSITIONS], U32, name="codes%d" % b, align_bytes=64) for b in range(SAMPLES)]
         scales = [keep.tile([P, POSITIONS], U8, name="scales%d" % b, align_bytes=64) for b in range(SAMPLES)]
@@ -83,13 +89,18 @@ def tile_block_height_reducing_filtering_pb_kernel(
         gain = [keep.tile([P, 1], F32, name="gain%d" % i) for i in range(OUT_TILES)]
         shift = [keep.tile([P, 1], F32, name="shift%d" % i) for i in range(OUT_TILES)]
 
-        def quantise(b):
-            grouped = keep.tile([P, POSITIONS * PACK], BF16, name="grouped%d" % b, align_bytes=64)
+        grouped = [
+            keep.tile([P, POSITIONS * PACK], BF16, name="grouped%d" % b, align_bytes=64) for b in range(SAMPLES)
+        ]
+
+        def regroup(b):
             by_run_in = raw[b][:].rearrange("p (t c i) -> p c t i", t=PACK, i=RUN)
-            by_run_out = grouped[:].rearrange("p (c i t) -> p c t i", i=RUN, t=PACK)
-            nc.vector.tensor_copy(out=by_run_out[:, 0 : RUNS // 2], in_=by_run_in[:, 0 : RUNS // 2])
-            nc.scalar.copy(out=by_run_out[:, RUNS // 2 : RUNS], in_=by_run_in[:, RUNS // 2 : RUNS])
-            nc.vector.quantize_mx(out=codes[b][:].bitcast(FP8X4), scales=scales[b][:], in_=grouped[:])
+            by_run_out = grouped[b][:].rearrange("p (c i t) -> p c t i", i=RUN, t=PACK)
+            nc.vector.tensor_copy(out=by_run_out[:, 0:VECTOR_RUNS], in_=by_run_in[:, 0:VECTOR_RUNS])
+            nc.scalar.copy(out=by_run_out[:, VECTOR_RUNS:RUNS], in_=by_run_in[:, VECTOR_RUNS:RUNS])
+
+        def quantise(b):
+            nc.vector.quantize_mx(out=codes[b][:].bitcast(FP8X4), scales=scales[b][:], in_=grouped[b][:])
 
         def multiply(i, b):
             banks[i, b] = psum.tile([P, POSITIONS], F32, tag="bank", name="m%d_%d" % (i, b))
@@ -138,12 +149,21 @@ def tile_block_height_reducing_filtering_pb_kernel(
             )
             nc.sync.dma_start(out=out[b, P * i : P * (i + 1), :], in_=result[:])
 
-        for b in range(SAMPLES):
-            quantise(b)
+        def multiply_first_tiles(b):
             for i in range(TILES_IN_PSUM):
                 multiply(i, b)
+
+        regroup(0)
+        for b in range(SAMPLES - 1):
+            regroup(b + 1)
+            quantise(b)
+            multiply_first_tiles(b)
             if b > 0:
                 statistics(0, b - 1)
+        nc.scalar.copy(out=gamma_beta[:], in_=gb_bank[:, 0 : 2 * OUT_TILES])
+        quantise(SAMPLES - 1)
+        multiply_first_tiles(SAMPLES - 1)
+        statistics(0, SAMPLES - 2)
         statistics(0, SAMPLES - 1)
         moments(0)
 

@@ -21,7 +21,9 @@ HEAD_PARTS = CHANNELS // PACK
 OUT_TILES = OUT_CHANNELS // P
 RUN = 4
 RUNS = POSITIONS // RUN
-VECTOR_RUNS = 48
+VECTOR_RUNS = 80
+PAIR = 2
+PORT_PARTS = 4
 STATS = 6
 PSUM_BANKS = 8
 TILES_IN_PSUM = PSUM_BANKS // SAMPLES
@@ -46,20 +48,20 @@ def tile_block_height_reducing_filtering_pb_kernel(
                 in_=W_merge_scales[0, 4 * quadrant : 4 * quadrant + 4, :].bitcast(I32),
             )
 
-        raw = [keep.tile([P, PACK * POSITIONS], BF16, name="raw%d" % b) for b in range(SAMPLES)]
-
-        def load(b):
-            for head in (0, 2, 1, 3):
-                nc.sync.dma_start(
-                    out=raw[b][HEAD_PARTS * head : HEAD_PARTS * (head + 1), :],
-                    in_=head_res[head, b].rearrange("(q t) d -> q (t d)", t=PACK),
-                )
-
-        load(0)
         w_words = keep.tile([P, 2 * OUT_CHANNELS], U8, align_bytes=64)
         nc.sync.dma_start(out=w_words[:].bitcast(I32), in_=W_merge_words[0].bitcast(I32))
-        for b in range(1, SAMPLES):
-            load(b)
+
+        raw = [keep.tile([P, PAIR, PACK * POSITIONS], BF16, name="raw%d" % u) for u in range(SAMPLES // PAIR)]
+        for u in range(SAMPLES // PAIR):
+            for head in range(HEADS):
+                by_port = head_res[head, PAIR * u : PAIR * (u + 1)].rearrange(
+                    "b (j r t) d -> r j b (t d)", r=PORT_PARTS, t=PACK
+                )
+                for r in range(PORT_PARTS):
+                    nc.sync.dma_start(
+                        out=raw[u][HEAD_PARTS * head + r : HEAD_PARTS * (head + 1) : PORT_PARTS],
+                        in_=by_port[r],
+                    )
 
         gb_rows = keep.tile([P, P], BF16)
         nc.vector.memset(gb_rows[:], 0.0)
@@ -94,7 +96,7 @@ def tile_block_height_reducing_filtering_pb_kernel(
         ]
 
         def regroup(b):
-            by_run_in = raw[b][:].rearrange("p (t c i) -> p c t i", t=PACK, i=RUN)
+            by_run_in = raw[b // PAIR][:, b % PAIR].rearrange("p (t c i) -> p c t i", t=PACK, i=RUN)
             by_run_out = grouped[b][:].rearrange("p (c i t) -> p c t i", i=RUN, t=PACK)
             nc.vector.tensor_copy(out=by_run_out[:, 0:VECTOR_RUNS], in_=by_run_in[:, 0:VECTOR_RUNS])
             nc.scalar.copy(out=by_run_out[:, VECTOR_RUNS:RUNS], in_=by_run_in[:, VECTOR_RUNS:RUNS])
@@ -153,18 +155,17 @@ def tile_block_height_reducing_filtering_pb_kernel(
             for i in range(TILES_IN_PSUM):
                 multiply(i, b)
 
-        regroup(0)
-        for b in range(SAMPLES - 1):
-            regroup(b + 1)
-            quantise(b)
-            multiply_first_tiles(b)
-            if b > 0:
-                statistics(0, b - 1)
-        nc.scalar.copy(out=gamma_beta[:], in_=gb_bank[:, 0 : 2 * OUT_TILES])
-        quantise(SAMPLES - 1)
-        multiply_first_tiles(SAMPLES - 1)
-        statistics(0, SAMPLES - 2)
-        statistics(0, SAMPLES - 1)
+        for u in range(SAMPLES // PAIR):
+            pair = range(PAIR * u, PAIR * (u + 1))
+            for b in pair:
+                regroup(b)
+            if u + 1 == SAMPLES // PAIR:
+                nc.scalar.copy(out=gamma_beta[:], in_=gb_bank[:, 0 : 2 * OUT_TILES])
+            for b in pair:
+                quantise(b)
+                multiply_first_tiles(b)
+            for b in pair:
+                statistics(0, b)
         moments(0)
 
         for i in range(OUT_TILES):

@@ -22,8 +22,6 @@ OUT_TILES = OUT_CHANNELS // P
 RUN = 4
 RUNS = POSITIONS // RUN
 VECTOR_RUNS = 80
-PAIR = 2
-PORT_PARTS = 4
 STATS = 6
 PSUM_BANKS = 8
 TILES_IN_PSUM = PSUM_BANKS // SAMPLES
@@ -40,6 +38,17 @@ def tile_block_height_reducing_filtering_pb_kernel(
         psum = ctx.enter_context(tc.psum_pool(name="psum", bufs=PSUM_BANKS))
         ctx.enter_context(tc.manual_schedule())
 
+        raw = [keep.tile([P, PACK * POSITIONS], BF16, name="raw%d" % b) for b in range(SAMPLES)]
+
+        def load(b):
+            for head in (0, 2, 1, 3):
+                nc.sync.dma_start(
+                    out=raw[b][HEAD_PARTS * head : HEAD_PARTS * (head + 1), :],
+                    in_=head_res[head, b].rearrange("(q t) d -> q (t d)", t=PACK),
+                )
+
+        load(0)
+
         w_scales = keep.tile([P, OUT_CHANNELS], U8, align_bytes=64)
         nc.vector.memset(w_scales[:].bitcast(I32), 0)
         for quadrant in range(4):
@@ -51,17 +60,8 @@ def tile_block_height_reducing_filtering_pb_kernel(
         w_words = keep.tile([P, 2 * OUT_CHANNELS], U8, align_bytes=64)
         nc.sync.dma_start(out=w_words[:].bitcast(I32), in_=W_merge_words[0].bitcast(I32))
 
-        raw = [keep.tile([P, PAIR, PACK * POSITIONS], BF16, name="raw%d" % u) for u in range(SAMPLES // PAIR)]
-        for u in range(SAMPLES // PAIR):
-            for head in range(HEADS):
-                by_port = head_res[head, PAIR * u : PAIR * (u + 1)].rearrange(
-                    "b (j r t) d -> r j b (t d)", r=PORT_PARTS, t=PACK
-                )
-                for r in range(PORT_PARTS):
-                    nc.sync.dma_start(
-                        out=raw[u][HEAD_PARTS * head + r : HEAD_PARTS * (head + 1) : PORT_PARTS],
-                        in_=by_port[r],
-                    )
+        for b in range(1, SAMPLES):
+            load(b)
 
         gb_rows = keep.tile([P, P], BF16)
         nc.vector.memset(gb_rows[:], 0.0)
@@ -96,7 +96,7 @@ def tile_block_height_reducing_filtering_pb_kernel(
         ]
 
         def regroup(b):
-            by_run_in = raw[b // PAIR][:, b % PAIR].rearrange("p (t c i) -> p c t i", t=PACK, i=RUN)
+            by_run_in = raw[b][:].rearrange("p (t c i) -> p c t i", t=PACK, i=RUN)
             by_run_out = grouped[b][:].rearrange("p (c i t) -> p c t i", i=RUN, t=PACK)
             nc.vector.tensor_copy(out=by_run_out[:, 0:VECTOR_RUNS], in_=by_run_in[:, 0:VECTOR_RUNS])
             nc.scalar.copy(out=by_run_out[:, VECTOR_RUNS:RUNS], in_=by_run_in[:, VECTOR_RUNS:RUNS])
@@ -155,17 +155,18 @@ def tile_block_height_reducing_filtering_pb_kernel(
             for i in range(TILES_IN_PSUM):
                 multiply(i, b)
 
-        for u in range(SAMPLES // PAIR):
-            pair = range(PAIR * u, PAIR * (u + 1))
-            for b in pair:
-                regroup(b)
-            if u + 1 == SAMPLES // PAIR:
-                nc.scalar.copy(out=gamma_beta[:], in_=gb_bank[:, 0 : 2 * OUT_TILES])
-            for b in pair:
-                quantise(b)
-                multiply_first_tiles(b)
-            for b in pair:
-                statistics(0, b)
+        for b in range(SAMPLES - 1):
+            regroup(b)
+            quantise(b)
+            multiply_first_tiles(b)
+            if b > 0:
+                statistics(0, b - 1)
+        regroup(SAMPLES - 1)
+        nc.scalar.copy(out=gamma_beta[:], in_=gb_bank[:, 0 : 2 * OUT_TILES])
+        quantise(SAMPLES - 1)
+        multiply_first_tiles(SAMPLES - 1)
+        statistics(0, SAMPLES - 2)
+        statistics(0, SAMPLES - 1)
         moments(0)
 
         for i in range(OUT_TILES):

@@ -21,7 +21,7 @@ HEAD_PARTS = CHANNELS // PACK
 OUT_TILES = OUT_CHANNELS // P
 RUN = 4
 RUNS = POSITIONS // RUN
-VECTOR_RUNS = 80
+VECTOR_RUNS = (80, 64, 64, 80)
 STATS = 6
 PSUM_BANKS = 8
 TILES_IN_PSUM = PSUM_BANKS // SAMPLES
@@ -73,8 +73,10 @@ def tile_block_height_reducing_filtering_pb_kernel(
         nc.vector.memset(identity[:], 0.0)
         make_identity(nc, identity[:], nomemset=True)
         gb_bank = psum.tile([P, P], BF16, tag="bank")
-        nc.tensor.transpose(gb_bank[:], gb_rows[:], identity[:])
-        gamma_beta = keep.tile([P, 2 * OUT_TILES], F32)
+        factors = keep.tile([P, OUT_TILES, 2], F32)
+        offsets = keep.tile([P, OUT_TILES, 2], F32)
+        gain_shift = keep.tile([P, OUT_TILES, 2], F32)
+        nc.vector.memset(offsets[:], 0.0)
 
         eps = keep.tile([P, 1], F32)
         nc.vector.memset(eps[:], EPS)
@@ -87,9 +89,6 @@ def tile_block_height_reducing_filtering_pb_kernel(
         stats = [keep.tile([P, SAMPLES * STATS], F32, name="stats%d" % i) for i in range(OUT_TILES)]
         mean_var = [keep.tile([P, 2], F32, name="mean_var%d" % i) for i in range(OUT_TILES)]
         rstd = [keep.tile([P, 1], F32, name="rstd%d" % i) for i in range(OUT_TILES)]
-        minus_mean_gamma = [keep.tile([P, 1], F32, name="minus_mean_gamma%d" % i) for i in range(OUT_TILES)]
-        gain = [keep.tile([P, 1], F32, name="gain%d" % i) for i in range(OUT_TILES)]
-        shift = [keep.tile([P, 1], F32, name="shift%d" % i) for i in range(OUT_TILES)]
 
         grouped = [
             keep.tile([P, POSITIONS * PACK], BF16, name="grouped%d" % b, align_bytes=64) for b in range(SAMPLES)
@@ -98,8 +97,9 @@ def tile_block_height_reducing_filtering_pb_kernel(
         def regroup(b):
             by_run_in = raw[b][:].rearrange("p (t c i) -> p c t i", t=PACK, i=RUN)
             by_run_out = grouped[b][:].rearrange("p (c i t) -> p c t i", i=RUN, t=PACK)
-            nc.vector.tensor_copy(out=by_run_out[:, 0:VECTOR_RUNS], in_=by_run_in[:, 0:VECTOR_RUNS])
-            nc.scalar.copy(out=by_run_out[:, VECTOR_RUNS:RUNS], in_=by_run_in[:, VECTOR_RUNS:RUNS])
+            split = VECTOR_RUNS[b]
+            nc.vector.tensor_copy(out=by_run_out[:, 0:split], in_=by_run_in[:, 0:split])
+            nc.scalar.copy(out=by_run_out[:, split:RUNS], in_=by_run_in[:, split:RUNS])
 
         def quantise(b):
             nc.vector.quantize_mx(out=codes[b][:].bitcast(FP8X4), scales=scales[b][:], in_=grouped[b][:])
@@ -119,27 +119,28 @@ def tile_block_height_reducing_filtering_pb_kernel(
         def statistics(i, b):
             nc.vector.bn_stats(out=stats[i][:, STATS * b : STATS * (b + 1)], in_=banks[i, b][:])
 
-        def moments(i):
-            nc.vector.bn_aggr(out=mean_var[i][:], in_=stats[i][:])
+        def root(i):
             nc.scalar.activation(
                 out=rstd[i][:], in_=mean_var[i][:, 1:2], func=ACT.Abs_reciprocal_sqrt, bias=eps[:], scale=1.0
             )
+
+        def aggregate(i):
+            nc.vector.bn_aggr(out=mean_var[i][:], in_=stats[i][:])
             nc.vector.tensor_scalar(
-                out=minus_mean_gamma[i][:],
+                out=factors[:, i, 1:2],
                 in0=mean_var[i][:, 0:1],
-                scalar1=gamma_beta[:, i : i + 1],
+                scalar1=factors[:, i, 0:1],
                 scalar2=-1.0,
                 op0=ALU.mult,
                 op1=ALU.mult,
             )
 
         def coefficients(i):
-            nc.vector.tensor_mul(out=gain[i][:], in0=rstd[i][:], in1=gamma_beta[:, i : i + 1])
-            nc.vector.tensor_scalar(
-                out=shift[i][:],
-                in0=rstd[i][:],
-                scalar1=minus_mean_gamma[i][:],
-                scalar2=gamma_beta[:, OUT_TILES + i : OUT_TILES + i + 1],
+            nc.vector.scalar_tensor_tensor(
+                out=gain_shift[:, i, :],
+                in0=factors[:, i, :],
+                scalar=rstd[i][:],
+                in1=offsets[:, i, :],
                 op0=ALU.mult,
                 op1=ALU.add,
             )
@@ -147,7 +148,11 @@ def tile_block_height_reducing_filtering_pb_kernel(
         def normalise(i, b):
             result = keep.tile([P, POSITIONS], F32, name="result%d_%d" % (i, b))
             nc.scalar.activation(
-                out=result[:], in_=banks[i, b][:], func=ACT.Relu, bias=shift[i][:], scale=gain[i][:]
+                out=result[:],
+                in_=banks[i, b][:],
+                func=ACT.Relu,
+                bias=gain_shift[:, i, 1:2],
+                scale=gain_shift[:, i, 0:1],
             )
             nc.sync.dma_start(out=out[b, P * i : P * (i + 1), :], in_=result[:])
 
@@ -155,30 +160,51 @@ def tile_block_height_reducing_filtering_pb_kernel(
             for i in range(TILES_IN_PSUM):
                 multiply(i, b)
 
-        for b in range(SAMPLES - 1):
+        def normalise_on_vector(i, b):
+            result = keep.tile([P, POSITIONS], F32, name="result%d_%d" % (i, b))
+            nc.vector.tensor_scalar(
+                out=result[:],
+                in0=banks[i, b][:],
+                scalar1=gain_shift[:, i, 0:1],
+                scalar2=gain_shift[:, i, 1:2],
+                op0=ALU.mult,
+                op1=ALU.add,
+            )
+            nc.vector.tensor_scalar_max(out=result[:], in0=result[:], scalar1=0.0)
+            nc.sync.dma_start(out=out[b, P * i : P * (i + 1), :], in_=result[:])
+
+        for b in range(SAMPLES):
             regroup(b)
-            quantise(b)
-            multiply_first_tiles(b)
+            if b == SAMPLES - 1:
+                nc.scalar.copy(out=factors[:, :, 0], in_=gb_bank[:, 0:OUT_TILES])
+                nc.scalar.copy(out=offsets[:, :, 1], in_=gb_bank[:, OUT_TILES : 2 * OUT_TILES])
             if b > 0:
                 statistics(0, b - 1)
-        regroup(SAMPLES - 1)
-        nc.scalar.copy(out=gamma_beta[:], in_=gb_bank[:, 0 : 2 * OUT_TILES])
-        quantise(SAMPLES - 1)
-        multiply_first_tiles(SAMPLES - 1)
-        statistics(0, SAMPLES - 2)
+            quantise(b)
+            multiply_first_tiles(b)
+            if b == 1:
+                nc.tensor.transpose(gb_bank[:], gb_rows[:], identity[:])
+        statistics(1, 0)
         statistics(0, SAMPLES - 1)
-        moments(0)
+        aggregate(0)
+        root(0)
 
         for i in range(OUT_TILES):
             following = i + 1
-            if following < OUT_TILES:
+            if following < OUT_TILES and i > 0:
                 statistics(following, 0)
+            if i == 0:
+                statistics(following, 1)
             coefficients(i)
             for b in range(SAMPLES):
-                normalise(i, b)
+                if following == OUT_TILES and b + 1 == SAMPLES:
+                    normalise_on_vector(i, b)
+                else:
+                    normalise(i, b)
                 if i + TILES_IN_PSUM < OUT_TILES:
                     multiply(i + TILES_IN_PSUM, b)
-                if following < OUT_TILES and b + 1 < SAMPLES:
+                if following < OUT_TILES and b + 1 < SAMPLES and (i > 0 or b > 0):
                     statistics(following, b + 1)
                 if following < OUT_TILES and b + 2 == SAMPLES:
-                    moments(following)
+                    aggregate(following)
+                    root(following)

@@ -21,8 +21,10 @@ HEAD_PARTS = CHANNELS // PACK
 OUT_TILES = OUT_CHANNELS // P
 RUN = 4
 RUNS = POSITIONS // RUN
-VECTOR_RUNS = (80, 64, 64, 80)
+VECTOR_RUNS = (80, 64, 64, 64)
+HALF = POSITIONS // 2
 STATS = 6
+TRIPLE = 3
 PSUM_BANKS = 8
 TILES_IN_PSUM = PSUM_BANKS // SAMPLES
 
@@ -86,7 +88,12 @@ def tile_block_height_reducing_filtering_pb_kernel(
         codes = [keep.tile([P, POSITIONS], U32, name="codes%d" % b, align_bytes=64) for b in range(SAMPLES)]
         scales = [keep.tile([P, POSITIONS], U8, name="scales%d" % b, align_bytes=64) for b in range(SAMPLES)]
         banks = {}
-        stats = [keep.tile([P, SAMPLES * STATS], F32, name="stats%d" % i) for i in range(OUT_TILES)]
+        stats_width = [SAMPLES * STATS] * OUT_TILES
+        stats_width[1] += TRIPLE - STATS
+        stats = [keep.tile([P, stats_width[i]], F32, name="stats%d" % i) for i in range(OUT_TILES)]
+        triple = stats[1][:, 0:TRIPLE]
+        nc.vector.memset(triple[:, 0:1], float(POSITIONS))
+        sums_dump = keep.tile([P, POSITIONS], F32)
         mean_var = [keep.tile([P, 2], F32, name="mean_var%d" % i) for i in range(OUT_TILES)]
         rstd = [keep.tile([P, 1], F32, name="rstd%d" % i) for i in range(OUT_TILES)]
 
@@ -101,23 +108,48 @@ def tile_block_height_reducing_filtering_pb_kernel(
             nc.vector.tensor_copy(out=by_run_out[:, 0:split], in_=by_run_in[:, 0:split])
             nc.scalar.copy(out=by_run_out[:, split:RUNS], in_=by_run_in[:, split:RUNS])
 
-        def quantise(b):
-            nc.vector.quantize_mx(out=codes[b][:].bitcast(FP8X4), scales=scales[b][:], in_=grouped[b][:])
+        def quantise(b, begin, end):
+            nc.vector.quantize_mx(
+                out=codes[b][:, begin:end].bitcast(FP8X4),
+                scales=scales[b][:, begin:end],
+                in_=grouped[b][:, PACK * begin : PACK * end],
+            )
 
-        def multiply(i, b):
-            banks[i, b] = psum.tile([P, POSITIONS], F32, tag="bank", name="m%d_%d" % (i, b))
+        def multiply(i, b, begin, end):
+            if begin == 0:
+                banks[i, b] = psum.tile([P, POSITIONS], F32, tag="bank", name="m%d_%d" % (i, b))
             nc.tensor.matmul_mx(
-                out=banks[i, b][:],
+                out=banks[i, b][:, begin:end],
                 lhsT=w_words[:, 2 * P * i : 2 * P * (i + 1)].bitcast(FP4X4),
                 lhsT_scale=w_scales[:, P * i : P * (i + 1)],
-                rhs=codes[b][:].bitcast(FP8X4),
-                rhs_scale=scales[b][:],
+                rhs=codes[b][:, begin:end].bitcast(FP8X4),
+                rhs_scale=scales[b][:, begin:end],
                 start=True,
                 stop=True,
             )
 
         def statistics(i, b):
-            nc.vector.bn_stats(out=stats[i][:, STATS * b : STATS * (b + 1)], in_=banks[i, b][:])
+            start = STATS * b
+            if i == 1:
+                start = TRIPLE if b == 0 else TRIPLE + STATS * (b - 1)
+            nc.vector.bn_stats(out=stats[i][:, start : start + STATS], in_=banks[i, b][:])
+
+        def scalar_statistics():
+            nc.scalar.activation(
+                out=sums_dump[:],
+                in_=banks[1, 1][:],
+                func=ACT.Identity,
+                scale=1.0 / POSITIONS,
+                accum_out=triple[:, 1:2],
+            )
+            nc.scalar.activation(
+                out=sums_dump[:],
+                in_=banks[1, 1][:],
+                func=ACT.Square,
+                scale=-1.0,
+                bias=triple[:, 1:2],
+                accum_out=triple[:, 2:3],
+            )
 
         def root(i):
             nc.scalar.activation(
@@ -145,64 +177,71 @@ def tile_block_height_reducing_filtering_pb_kernel(
                 op1=ALU.add,
             )
 
-        def normalise(i, b):
-            result = keep.tile([P, POSITIONS], F32, name="result%d_%d" % (i, b))
+        def normalise(i, b, begin, end):
+            result = keep.tile([P, end - begin], F32, name="result%d_%d_%d" % (i, b, begin))
             nc.scalar.activation(
                 out=result[:],
-                in_=banks[i, b][:],
+                in_=banks[i, b][:, begin:end],
                 func=ACT.Relu,
                 bias=gain_shift[:, i, 1:2],
                 scale=gain_shift[:, i, 0:1],
             )
-            nc.sync.dma_start(out=out[b, P * i : P * (i + 1), :], in_=result[:])
+            nc.sync.dma_start(out=out[b, P * i : P * (i + 1), begin:end], in_=result[:])
 
-        def multiply_first_tiles(b):
-            for i in range(TILES_IN_PSUM):
-                multiply(i, b)
-
-        def normalise_on_vector(i, b):
-            result = keep.tile([P, POSITIONS], F32, name="result%d_%d" % (i, b))
+        def normalise_on_vector(i, b, begin, end):
+            result = keep.tile([P, end - begin], F32, name="result%d_%d_%d" % (i, b, begin))
             nc.vector.tensor_scalar(
                 out=result[:],
-                in0=banks[i, b][:],
+                in0=banks[i, b][:, begin:end],
                 scalar1=gain_shift[:, i, 0:1],
                 scalar2=gain_shift[:, i, 1:2],
                 op0=ALU.mult,
                 op1=ALU.add,
             )
             nc.vector.tensor_scalar_max(out=result[:], in0=result[:], scalar1=0.0)
-            nc.sync.dma_start(out=out[b, P * i : P * (i + 1), :], in_=result[:])
+            nc.sync.dma_start(out=out[b, P * i : P * (i + 1), begin:end], in_=result[:])
 
-        for b in range(SAMPLES):
+        last = SAMPLES - 1
+        for b in range(last):
             regroup(b)
-            if b == SAMPLES - 1:
-                nc.scalar.copy(out=factors[:, :, 0], in_=gb_bank[:, 0:OUT_TILES])
-                nc.scalar.copy(out=offsets[:, :, 1], in_=gb_bank[:, OUT_TILES : 2 * OUT_TILES])
             if b > 0:
                 statistics(0, b - 1)
-            quantise(b)
-            multiply_first_tiles(b)
+            quantise(b, 0, POSITIONS)
+            for i in range(TILES_IN_PSUM):
+                multiply(i, b, 0, POSITIONS)
             if b == 1:
+                statistics(1, 0)
                 nc.tensor.transpose(gb_bank[:], gb_rows[:], identity[:])
-        statistics(1, 0)
-        statistics(0, SAMPLES - 1)
+        regroup(last)
+        nc.scalar.copy(out=factors[:, :, 0], in_=gb_bank[:, 0:OUT_TILES])
+        nc.scalar.copy(out=offsets[:, :, 1], in_=gb_bank[:, OUT_TILES : 2 * OUT_TILES])
+        for half in range(2):
+            quantise(last, HALF * half, HALF * (half + 1))
+        for i in range(TILES_IN_PSUM):
+            for half in range(2):
+                multiply(i, last, HALF * half, HALF * (half + 1))
+        scalar_statistics()
+        statistics(0, last - 1)
+        statistics(0, last)
         aggregate(0)
         root(0)
+        coefficients(0)
 
         for i in range(OUT_TILES):
             following = i + 1
-            if following < OUT_TILES and i > 0:
+            if 0 < i and following < OUT_TILES:
                 statistics(following, 0)
-            if i == 0:
-                statistics(following, 1)
-            coefficients(i)
+            if i > 0:
+                coefficients(i)
             for b in range(SAMPLES):
-                if following == OUT_TILES and b + 1 == SAMPLES:
-                    normalise_on_vector(i, b)
-                else:
-                    normalise(i, b)
+                if following == OUT_TILES and b == last - 1:
+                    normalise_on_vector(i, last, 0, POSITIONS)
+                    normalise(i, b, 0, HALF)
+                    normalise_on_vector(i, b, HALF, POSITIONS)
+                elif following < OUT_TILES or b < last:
+                    normalise(i, b, 0, POSITIONS)
                 if i + TILES_IN_PSUM < OUT_TILES:
-                    multiply(i + TILES_IN_PSUM, b)
+                    multiply(i + TILES_IN_PSUM, b, 0, POSITIONS)
                 if following < OUT_TILES and b + 1 < SAMPLES and (i > 0 or b > 0):
                     statistics(following, b + 1)
                 if following < OUT_TILES and b + 2 == SAMPLES:

@@ -21,7 +21,7 @@ HEAD_PARTS = CHANNELS // PACK
 OUT_TILES = OUT_CHANNELS // P
 RUN = 4
 RUNS = POSITIONS // RUN
-VECTOR_RUNS = (80, 64, 64, 64)
+VECTOR_RUNS = (80, 64, 64, 80)
 HALF = POSITIONS // 2
 STATS = 6
 TRIPLE = 3
@@ -105,7 +105,9 @@ def tile_block_height_reducing_filtering_pb_kernel(
             by_run_in = raw[b][:].rearrange("p (t c i) -> p c t i", t=PACK, i=RUN)
             by_run_out = grouped[b][:].rearrange("p (c i t) -> p c t i", i=RUN, t=PACK)
             split = VECTOR_RUNS[b]
-            nc.vector.tensor_copy(out=by_run_out[:, 0:split], in_=by_run_in[:, 0:split])
+            begins = (0, split) if b < SAMPLES - 1 else (0, RUNS // 2, split)
+            for begin, end in zip(begins, begins[1:]):
+                nc.vector.tensor_copy(out=by_run_out[:, begin:end], in_=by_run_in[:, begin:end])
             nc.scalar.copy(out=by_run_out[:, split:RUNS], in_=by_run_in[:, split:RUNS])
 
         def quantise(b, begin, end):
@@ -188,7 +190,7 @@ def tile_block_height_reducing_filtering_pb_kernel(
             )
             nc.sync.dma_start(out=out[b, P * i : P * (i + 1), begin:end], in_=result[:])
 
-        def normalise_on_vector(i, b, begin, end):
+        def affine_on_vector(i, b, begin, end):
             result = keep.tile([P, end - begin], F32, name="result%d_%d_%d" % (i, b, begin))
             nc.vector.tensor_scalar(
                 out=result[:],
@@ -198,6 +200,9 @@ def tile_block_height_reducing_filtering_pb_kernel(
                 op0=ALU.mult,
                 op1=ALU.add,
             )
+            return result
+
+        def relu_on_vector(i, b, begin, end, result):
             nc.vector.tensor_scalar_max(out=result[:], in0=result[:], scalar1=0.0)
             nc.sync.dma_start(out=out[b, P * i : P * (i + 1), begin:end], in_=result[:])
 
@@ -235,9 +240,14 @@ def tile_block_height_reducing_filtering_pb_kernel(
                 coefficients(i)
             for b in range(SAMPLES):
                 if following == OUT_TILES and b == last - 1:
-                    normalise_on_vector(i, last, 0, POSITIONS)
+                    whole = affine_on_vector(i, last, 0, POSITIONS)
+                    half = affine_on_vector(i, b, HALF, POSITIONS)
+                    relu_on_vector(i, last, 0, POSITIONS, whole)
                     normalise(i, b, 0, HALF)
-                    normalise_on_vector(i, b, HALF, POSITIONS)
+                    relu_on_vector(i, b, HALF, POSITIONS, half)
+                elif i == 0 and b == 0:
+                    normalise(i, b, 0, HALF)
+                    normalise(i, b, HALF, POSITIONS)
                 elif following < OUT_TILES or b < last:
                     normalise(i, b, 0, POSITIONS)
                 if i + TILES_IN_PSUM < OUT_TILES:

from contextlib import ExitStack

import concourse.mybir as mybir
from concourse.masks import make_identity

F32 = mybir.dt.float32
BF16 = mybir.dt.bfloat16
I32 = mybir.dt.int32
U32 = mybir.dt.uint32
U8 = mybir.dt.uint8
FP8X4 = mybir.dt.float8_e4m3fn_x4
FP4X4 = mybir.dt.float4_e2m1fn_x4
ACT = mybir.ActivationFunctionType
ALU = mybir.AluOpType

HEADS, SAMPLES, CHANNELS, POSITIONS, OUT_CHANNELS = 4, 4, 128, 512, 512
EPS = 1e-5
P = 128
PACK = 4
HEAD_PARTS = CHANNELS // PACK
OUT_TILES = OUT_CHANNELS // P
RUN = 4
RUNS = POSITIONS // RUN
VECTOR_RUNS = (80, 64, 64, 80)
HALF = POSITIONS // 2
STATS = 6
TRIPLE = 3
PSUM_BANKS = 8
TILES_IN_PSUM = PSUM_BANKS // SAMPLES

FLOPS = 2 * SAMPLES * OUT_CHANNELS * HEADS * CHANNELS * POSITIONS


def tile_block_height_reducing_filtering_pb_kernel(
    tc, head_res, W_merge_words, W_merge_scales, g_m, b_m, out
):
    nc = tc.nc
    with ExitStack() as ctx:
        keep = ctx.enter_context(tc.tile_pool(name="keep", bufs=1))
        psum = ctx.enter_context(tc.psum_pool(name="psum", bufs=PSUM_BANKS))
        ctx.enter_context(tc.manual_schedule())

        raw = [keep.tile([P, PACK * POSITIONS], BF16, name="raw%d" % b) for b in range(SAMPLES)]

        def load(b):
            for head in (0, 2, 1, 3):
                nc.sync.dma_start(
                    out=raw[b][HEAD_PARTS * head : HEAD_PARTS * (head + 1), :],
                    in_=head_res[head, b].rearrange("(q t) d -> q (t d)", t=PACK),
                )

        load(0)

        w_scales = keep.tile([P, OUT_CHANNELS], U8, align_bytes=64)
        nc.vector.memset(w_scales[:].bitcast(I32), 0)
        for quadrant in range(4):
            nc.sync.dma_start(
                out=w_scales[32 * quadrant : 32 * quadrant + 4, :].bitcast(I32),
                in_=W_merge_scales[0, 4 * quadrant : 4 * quadrant + 4, :].bitcast(I32),
            )

        w_words = keep.tile([P, 2 * OUT_CHANNELS], U8, align_bytes=64)
        nc.sync.dma_start(out=w_words[:].bitcast(I32), in_=W_merge_words[0].bitcast(I32))

        for b in range(1, SAMPLES):
            load(b)

        gb_rows = keep.tile([P, P], BF16)
        nc.vector.memset(gb_rows[:], 0.0)
        nc.gpsimd.dma_start(out=gb_rows[0:OUT_TILES, :], in_=g_m.rearrange("(i c) -> i c", c=P))
        nc.gpsimd.dma_start(
            out=gb_rows[OUT_TILES : 2 * OUT_TILES, :], in_=b_m.rearrange("(i c) -> i c", c=P)
        )
        identity = keep.tile([P, P], BF16)
        nc.vector.memset(identity[:], 0.0)
        make_identity(nc, identity[:], nomemset=True)
        gb_bank = psum.tile([P, P], BF16, tag="bank")
        factors = keep.tile([P, OUT_TILES, 2], F32)
        offsets = keep.tile([P, OUT_TILES, 2], F32)
        gain_shift = keep.tile([P, OUT_TILES, 2], F32)
        nc.vector.memset(offsets[:], 0.0)

        eps = keep.tile([P, 1], F32)
        nc.vector.memset(eps[:], EPS)
        table_warmer = keep.tile([P, 1], F32)
        nc.scalar.activation(out=table_warmer[:], in_=eps[:], func=ACT.Abs_reciprocal_sqrt)

        codes = [keep.tile([P, POSITIONS], U32, name="codes%d" % b, align_bytes=64) for b in range(SAMPLES)]
        scales = [keep.tile([P, POSITIONS], U8, name="scales%d" % b, align_bytes=64) for b in range(SAMPLES)]
        banks = {}
        stats_width = [SAMPLES * STATS] * OUT_TILES
        stats_width[1] += TRIPLE - STATS
        stats = [keep.tile([P, stats_width[i]], F32, name="stats%d" % i) for i in range(OUT_TILES)]
        triple = stats[1][:, 0:TRIPLE]
        nc.vector.memset(triple[:, 0:1], float(POSITIONS))
        sums_dump = keep.tile([P, POSITIONS], F32)
        mean_var = [keep.tile([P, 2], F32, name="mean_var%d" % i) for i in range(OUT_TILES)]
        rstd = [keep.tile([P, 1], F32, name="rstd%d" % i) for i in range(OUT_TILES)]

        grouped = [
            keep.tile([P, POSITIONS * PACK], BF16, name="grouped%d" % b, align_bytes=64) for b in range(SAMPLES)
        ]

        def regroup(b):
            by_run_in = raw[b][:].rearrange("p (t c i) -> p c t i", t=PACK, i=RUN)
            by_run_out = grouped[b][:].rearrange("p (c i t) -> p c t i", i=RUN, t=PACK)
            split = VECTOR_RUNS[b]
            begins = (0, split) if b < SAMPLES - 1 else (0, RUNS // 2, split)
            for begin, end in zip(begins, begins[1:]):
                nc.vector.tensor_copy(out=by_run_out[:, begin:end], in_=by_run_in[:, begin:end])
            nc.scalar.copy(out=by_run_out[:, split:RUNS], in_=by_run_in[:, split:RUNS])

        def quantise(b, begin, end):
            nc.vector.quantize_mx(
                out=codes[b][:, begin:end].bitcast(FP8X4),
                scales=scales[b][:, begin:end],
                in_=grouped[b][:, PACK * begin : PACK * end],
            )

        def multiply(i, b, begin, end):
            if begin == 0:
                banks[i, b] = psum.tile([P, POSITIONS], F32, tag="bank", name="m%d_%d" % (i, b))
            nc.tensor.matmul_mx(
                out=banks[i, b][:, begin:end],
                lhsT=w_words[:, 2 * P * i : 2 * P * (i + 1)].bitcast(FP4X4),
                lhsT_scale=w_scales[:, P * i : P * (i + 1)],
                rhs=codes[b][:, begin:end].bitcast(FP8X4),
                rhs_scale=scales[b][:, begin:end],
                start=True,
                stop=True,
            )

        def statistics(i, b):
            start = STATS * b
            if i == 1:
                start = TRIPLE if b == 0 else TRIPLE + STATS * (b - 1)
            nc.vector.bn_stats(out=stats[i][:, start : start + STATS], in_=banks[i, b][:])

        def scalar_statistics():
            nc.scalar.activation(
                out=sums_dump[:],
                in_=banks[1, 1][:],
                func=ACT.Identity,
                scale=1.0 / POSITIONS,
                accum_out=triple[:, 1:2],
            )
            nc.scalar.activation(
                out=sums_dump[:],
                in_=banks[1, 1][:],
                func=ACT.Square,
                scale=-1.0,
                bias=triple[:, 1:2],
                accum_out=triple[:, 2:3],
            )

        def root(i):
            nc.scalar.activation(
                out=rstd[i][:], in_=mean_var[i][:, 1:2], func=ACT.Abs_reciprocal_sqrt, bias=eps[:], scale=1.0
            )

        def aggregate(i):
            nc.vector.bn_aggr(out=mean_var[i][:], in_=stats[i][:])
            nc.vector.tensor_scalar(
                out=factors[:, i, 1:2],
                in0=mean_var[i][:, 0:1],
                scalar1=factors[:, i, 0:1],
                scalar2=-1.0,
                op0=ALU.mult,
                op1=ALU.mult,
            )

        def coefficients(i):
            nc.vector.scalar_tensor_tensor(
                out=gain_shift[:, i, :],
                in0=factors[:, i, :],
                scalar=rstd[i][:],
                in1=offsets[:, i, :],
                op0=ALU.mult,
                op1=ALU.add,
            )

        def normalise(i, b, begin, end):
            result = keep.tile([P, end - begin], F32, name="result%d_%d_%d" % (i, b, begin))
            nc.scalar.activation(
                out=result[:],
                in_=banks[i, b][:, begin:end],
                func=ACT.Relu,
                bias=gain_shift[:, i, 1:2],
                scale=gain_shift[:, i, 0:1],
            )
            nc.sync.dma_start(out=out[b, P * i : P * (i + 1), begin:end], in_=result[:])

        def affine_on_vector(i, b, begin, end):
            result = keep.tile([P, end - begin], F32, name="result%d_%d_%d" % (i, b, begin))
            nc.vector.tensor_scalar(
                out=result[:],
                in0=banks[i, b][:, begin:end],
                scalar1=gain_shift[:, i, 0:1],
                scalar2=gain_shift[:, i, 1:2],
                op0=ALU.mult,
                op1=ALU.add,
            )
            return result

        def relu_on_vector(i, b, begin, end, result):
            nc.vector.tensor_scalar_max(out=result[:], in0=result[:], scalar1=0.0)
            nc.sync.dma_start(out=out[b, P * i : P * (i + 1), begin:end], in_=result[:])

        last = SAMPLES - 1
        for b in range(last):
            regroup(b)
            if b > 0:
                statistics(0, b - 1)
            quantise(b, 0, POSITIONS)
            for i in range(TILES_IN_PSUM):
                multiply(i, b, 0, POSITIONS)
            if b == 1:
                statistics(1, 0)
                nc.tensor.transpose(gb_bank[:], gb_rows[:], identity[:])
        regroup(last)
        nc.scalar.copy(out=factors[:, :, 0], in_=gb_bank[:, 0:OUT_TILES])
        nc.scalar.copy(out=offsets[:, :, 1], in_=gb_bank[:, OUT_TILES : 2 * OUT_TILES])
        for half in range(2):
            quantise(last, HALF * half, HALF * (half + 1))
        for i in range(TILES_IN_PSUM):
            for half in range(2):
                multiply(i, last, HALF * half, HALF * (half + 1))
        scalar_statistics()
        statistics(0, last - 1)
        statistics(0, last)
        aggregate(0)
        root(0)
        coefficients(0)

        for i in range(OUT_TILES):
            following = i + 1
            if 0 < i and following < OUT_TILES:
                statistics(following, 0)
            if i > 0:
                coefficients(i)
            for b in range(SAMPLES):
                if following == OUT_TILES and b == last - 1:
                    whole = affine_on_vector(i, last, 0, POSITIONS)
                    half = affine_on_vector(i, b, HALF, POSITIONS)
                    relu_on_vector(i, last, 0, POSITIONS, whole)
                    normalise(i, b, 0, HALF)
                    relu_on_vector(i, b, HALF, POSITIONS, half)
                elif i == 0 and b == 0:
                    normalise(i, b, 0, HALF)
                    normalise(i, b, HALF, POSITIONS)
                elif following < OUT_TILES or b < last:
                    normalise(i, b, 0, POSITIONS)
                if i + TILES_IN_PSUM < OUT_TILES:
                    multiply(i + TILES_IN_PSUM, b, 0, POSITIONS)
                if following < OUT_TILES and b + 1 < SAMPLES and (i > 0 or b > 0):
                    statistics(following, b + 1)
                if following < OUT_TILES and b + 2 == SAMPLES:
                    aggregate(following)
                    root(following)
